import numpy as np
import ml_dtypes


def mxq(x, axis, fmt="e4m3"):
    dtype, down = {"e4m3": (ml_dtypes.float8_e4m3fn, 7), "e5m2": (ml_dtypes.float8_e5m2, 14)}[fmt]
    v = np.moveaxis(np.asarray(x, np.float32).astype(ml_dtypes.bfloat16).astype(np.float64), axis, -1)
    blocks = v.reshape(v.shape[:-1] + (-1, 32))
    amax = np.abs(blocks).max(-1, keepdims=True)
    byte = np.maximum(np.where(amax > 0, np.frexp(amax)[1] - 1 + 127, 0) - down, 1)
    scale = np.exp2(byte - 127.0)
    codes = (blocks / scale).astype(np.float32).astype(dtype).astype(np.float64)
    return np.moveaxis((codes * scale).reshape(v.shape), -1, axis)


WIDE = False


def mx_kscale(k):
    if not WIDE:
        return np.ones(k)
    levels = np.array([10, -10, 5, -5, 0])
    a = np.random.permutation(np.resize(levels, k // 512 * 4)).reshape(k // 512, 4)
    idx = np.arange(k)
    return np.exp2(a[idx // 512, idx % 128 // 32])


BF16 = ml_dtypes.bfloat16


def bf(x):
    return np.asarray(x, np.float32).astype(BF16)


def f64(x):
    return np.asarray(x).astype(np.float64)


B, C, CO, H, W = 2, 2048, 512, 24, 24
EPS = 1e-5
POOL_SIZES = (1, 2, 3, 6)
N = H * W


def bn_relu(y, scale, bias, mean, var):
    inv = scale / np.sqrt(var + EPS)
    return np.maximum((y - mean[None, :, None]) * inv[None, :, None] + bias[None, :, None], 0.0)


def pyramid_pool(f):
    feats = []
    for s in POOL_SIZES:
        p = f.reshape(B, CO, s, H // s, s, W // s).mean(axis=(3, 5))
        feats.append(p.reshape(B, CO, s * s))
    return np.concatenate(feats, axis=-1)


def setup_inputs():
    s = mx_kscale(C)
    d = {}
    d["x"] = bf(np.random.standard_normal((B, C, H, W)) * s[None, :, None, None])
    for n in ("q", "k"):
        d["w" + n] = bf(np.random.standard_normal((CO, C)) * 0.5 / np.sqrt(C) / s[None, :])
        d[n + "_scale"] = bf(np.random.uniform(0.5, 1.5, CO))
        d[n + "_bias"] = bf(np.random.standard_normal(CO) * 0.1)
        d[n + "_mean"] = bf(np.random.standard_normal(CO) * 0.1)
        d[n + "_var"] = bf(np.random.uniform(0.5, 1.5, CO))
    return d


def reference(x, wq, q_scale, q_bias, q_mean, q_var, wk, k_scale, k_bias, k_mean, k_var):
    xq = mxq(f64(x).reshape(B, C, N), 1, "e4m3")
    yq = mxq(f64(wq), 1, "e4m3") @ xq
    yk = mxq(f64(wk), 1, "e4m3") @ xq
    q = pyramid_pool(bn_relu(yq, f64(q_scale), f64(q_bias), f64(q_mean), f64(q_var)))
    k = pyramid_pool(bn_relu(yk, f64(k_scale), f64(k_bias), f64(k_mean), f64(k_var)))
    return q, k

@@ -1,0 +1,261 @@
+from contextlib import ExitStack
+
+import concourse.mybir as mybir
+from concourse.masks import make_identity
+
+FLOPS = 2 * 2 * 2 * 512 * 2048 * 576
+
+FP8X4 = mybir.dt.float8_e4m3fn_x4
+BF16 = mybir.dt.bfloat16
+F32 = mybir.dt.float32
+U32 = mybir.dt.uint32
+U8 = mybir.dt.uint8
+ALU = mybir.AluOpType
+ACT = mybir.ActivationFunctionType
+AX = mybir.AxisListType
+
+P = 128
+EPS = 1e-5
+NPOS = 576
+PIN = False
+CS = (192, 128)
+WXV = (4, 5, 6, 7)
+
+
+def tile_guided_cam_module2_pa_kernel(
+    tc, x, wq, q_scale, q_bias, q_mean, q_var, wk, k_scale, k_bias, k_mean, k_var, out_0, out_1
+):
+    nc = tc.nc
+    with ExitStack() as ctx:
+        keep = ctx.enter_context(tc.tile_pool(name="keep", bufs=1))
+        wgrp_pool = ctx.enter_context(tc.tile_pool(name="wgrp", bufs=3))
+        xgrp_pool = ctx.enter_context(tc.tile_pool(name="xgrp", bufs=3))
+        psum = ctx.enter_context(tc.psum_pool(name="psum", bufs=8))
+        if PIN:
+            ctx.enter_context(tc.manual_schedule())
+
+        xv = x.rearrange("b (g u p e) h w -> b g p u (e h w)", g=4, u=2, p=P, e=2)
+        wv = [wq.rearrange("(p t) k -> p t k", t=4), wk.rearrange("(p t) k -> p t k", t=4)]
+        wraw = []
+        xraw = []
+        for i in range(8):
+            wt = keep.tile([P, 2048], BF16, name="wraw%d" % i)
+            nc.sync.dma_start(out=wt[:], in_=wv[i // 4][:, i % 4, :])
+            wraw.append(wt)
+            xt = keep.tile([P, 2, 2 * NPOS], BF16, name="xraw%d" % i)
+            nc.sync.dma_start(out=xt[:], in_=xv[i // 4, i % 4])
+            xraw.append(xt)
+
+        bnraw = keep.tile([P, 8, 16], BF16, name="bnraw")
+        for v, vec in enumerate((q_scale, k_scale, q_bias, k_bias, q_mean, k_mean, q_var, k_var)):
+            nc.scalar.dma_start(out=bnraw[:, v, 0:4], in_=vec.rearrange("(p t) -> p t", t=4))
+
+        ident = keep.tile([P, P], F32, name="ident")
+        make_identity(nc, ident[:])
+
+        warm = keep.tile([P, 2], F32, name="warm")
+        nc.vector.memset(warm[:, 0:1], 1.0)
+        nc.scalar.sqrt(warm[:, 1:2], warm[:, 0:1])
+
+        wc = [keep.tile([P, 512], U32, name="wc%d" % m, align_bytes=64) for m in range(8)]
+        ws = [keep.tile([P, 512], U8, name="ws%d" % m, align_bytes=64) for m in range(8)]
+        xc = [keep.tile([P, 1152], U32, name="xc%d" % g, align_bytes=64) for g in range(4)]
+        xs = [keep.tile([P, 1152], U8, name="xs%d" % g, align_bytes=64) for g in range(4)]
+        z = [keep.tile([P, 2, NPOS], F32, name="z%d" % m) for m in range(8)]
+        l6 = keep.tile([P, 8, 2, 36], F32, name="l6")
+        res = [keep.tile([P, 2, 4, 50], F32, name="res%d" % br) for br in range(2)]
+        a16 = keep.tile([P, 8], F32, name="a16")
+        c16 = keep.tile([P, 8], F32, name="c16")
+
+        def bn_prepare():
+            bn32 = keep.tile([P, 8, 4], F32, name="bn32")
+            nc.vector.tensor_copy(out=bn32[:], in_=bnraw[:, :, 0:4])
+            flat = bn32[:].rearrange("p v t -> p (v t)")
+            sd = keep.tile([P, 8], F32, name="sd")
+            nc.vector.tensor_scalar_add(out=sd[:], in0=flat[:, 24:32], scalar1=EPS)
+            nc.scalar.sqrt(sd[:], sd[:])
+            rstd = keep.tile([P, 8], F32, name="rstd")
+            nc.vector.reciprocal(out=rstd[:], in_=sd[:])
+            nc.vector.scalar_tensor_tensor(
+                out=a16[:], in0=flat[:, 0:8], scalar=1.0 / 16.0, in1=rstd[:], op0=ALU.mult, op1=ALU.mult
+            )
+            ma = keep.tile([P, 8], F32, name="ma")
+            nc.vector.tensor_mul(out=ma[:], in0=flat[:, 16:24], in1=a16[:])
+            nc.vector.scalar_tensor_tensor(
+                out=c16[:], in0=flat[:, 8:16], scalar=1.0 / 16.0, in1=ma[:], op0=ALU.mult, op1=ALU.subtract
+            )
+
+        tps = {}
+        wgs = {}
+        xgs = {}
+        ys = {}
+
+        def transposes(m):
+            w32 = wraw[m][:].bitcast(F32)
+            for h in range(2):
+                tp = psum.tile([P, 4, P], F32, name="tp%d_%d" % (m, h), tag="bank")
+                for j in range(4):
+                    blk = 4 * h + j
+                    nc.tensor.transpose(tp[:, j, :], w32[:, P * blk : P * (blk + 1)], ident[:])
+                tps[(m, h)] = tp
+
+        def w_out(m):
+            wg = wgrp_pool.tile([P, 2048], BF16, name="wg%d" % m, tag="wg", align_bytes=64)
+            wgs[m] = wg
+            wg32 = wg[:].bitcast(F32).rearrange("p (g c u) -> p g c u", g=4, c=P, u=2)
+            for h in range(2):
+                src = tps[(m, h)][:].rearrange("p (g u) c -> p g c u", u=2)
+                dst = wg32[:, 2 * h : 2 * h + 2, :, :]
+                if h == 1 and m in WXV:
+                    nc.vector.tensor_copy(out=dst, in_=src)
+                else:
+                    nc.scalar.copy(out=dst, in_=src)
+
+        def w_quant(m):
+            nc.vector.quantize_mx(out=wc[m][:].bitcast(FP8X4), scales=ws[m][:], in_=wgs[m][:])
+
+        def x_regroup(i, engine):
+            b = i // 4
+            if i not in xgs:
+                xgs[i] = xgrp_pool.tile([P, NPOS, 4], BF16, name="xg%d" % i, tag="xg", align_bytes=64)
+            cv = NPOS - CS[b]
+            lo, hi = (0, cv) if engine == "v" else (cv, NPOS)
+            if lo == hi:
+                return
+            src = xraw[i][:].rearrange("p u (e n) -> p (u e) n", e=2)[:, :, lo:hi]
+            src = src.rearrange("p t (c i) -> p c t i", i=4)
+            dst = xgs[i][:, lo:hi, :].rearrange("p (c i) t -> p c t i", i=4)
+            if engine == "v":
+                nc.vector.tensor_copy(out=dst, in_=src)
+            else:
+                nc.scalar.copy(out=dst, in_=src)
+
+        def x_quant(i):
+            b, g = i // 4, i % 4
+            flat = xgs[i][:].rearrange("p c t -> p (c t)")
+            nc.vector.quantize_mx(
+                out=xc[g][:, 512 * b : 512 * b + 512].bitcast(FP8X4),
+                scales=xs[g][:, 512 * b : 512 * b + 512],
+                in_=flat[:, 0:2048],
+            )
+            nc.vector.quantize_mx(
+                out=xc[g][:, 1024 + 64 * b : 1088 + 64 * b].bitcast(FP8X4),
+                scales=xs[g][:, 1024 + 64 * b : 1088 + 64 * b],
+                in_=flat[:, 2048:2304],
+            )
+
+        def mx(c, m, g):
+            lo, n = ((0, 512), (512, 512), (1024, 128))[c]
+            if g == 0:
+                ys[(c, m)] = psum.tile([P, n], F32, name="y%d_%d" % (c, m), tag="bank")
+            nc.tensor.matmul_mx(
+                out=ys[(c, m)][:],
+                lhsT=wc[m][:, P * g : P * (g + 1)].bitcast(FP8X4),
+                lhsT_scale=ws[m][:, P * g : P * (g + 1)],
+                rhs=xc[g][:, lo : lo + n].bitcast(FP8X4),
+                rhs_scale=xs[g][:, lo : lo + n],
+                start=(g == 0),
+                stop=(g == 3),
+            )
+
+        def y_out(c, m):
+            if c < 2:
+                dst = z[m][:, c, 0:512]
+                src = ys[(c, m)][:]
+            else:
+                dst = z[m][:, :, 512:NPOS]
+                src = ys[(c, m)][:].rearrange("p (b n) -> p b n", b=2)
+            nc.scalar.activation(
+                out=dst, in_=src, func=ACT.Relu, bias=c16[:, m : m + 1], scale=a16[:, m : m + 1]
+            )
+
+        def pool(c, m):
+            if c < 2:
+                src = z[m][:, c, 0:480].rearrange("p (hb hi wb wi) -> p hb wb hi wi", hb=5, hi=4, wb=6, wi=4)
+                dst = l6[:, m, c, 0:30].rearrange("p (hb wb) -> p hb wb", wb=6)
+            else:
+                src = z[m][:, :, 480:NPOS].rearrange("p b (hi wb wi) -> p b wb hi wi", hi=4, wb=6, wi=4)
+                dst = l6[:, m, :, 30:36]
+            nc.vector.tensor_reduce(out=dst, in_=src, axis=AX.XY, op=ALU.add)
+
+        def finish(br):
+            m0 = 4 * br
+            part = l6[:, m0 : m0 + 4, :, :]
+            out_view = res[br][:].rearrange("p b t f -> p t b f")
+            nc.scalar.copy(out=out_view[:, :, :, 14:50], in_=part)
+            s3 = keep.tile([P, 24, 3], F32, name="s3_%d" % br)
+            nc.vector.tensor_reduce(
+                out=s3[:],
+                in_=part.rearrange("p m b (i di j dj) -> p (m b i) j di dj", i=3, di=2, j=3, dj=2),
+                axis=AX.XY,
+                op=ALU.add,
+            )
+            nc.scalar.mul(
+                out_view[:, :, :, 5:14], s3[:].rearrange("p (m b i) j -> p m b (i j)", m=4, b=2), 0.25
+            )
+            s2 = keep.tile([P, 16, 2], F32, name="s2_%d" % br)
+            nc.vector.tensor_reduce(
+                out=s2[:],
+                in_=part.rearrange("p m b (i di j dj) -> p (m b i) j di dj", i=2, di=3, j=2, dj=3),
+                axis=AX.XY,
+                op=ALU.add,
+            )
+            nc.scalar.mul(
+                out_view[:, :, :, 1:5], s2[:].rearrange("p (m b i) j -> p m b (i j)", m=4, b=2), 1.0 / 9.0
+            )
+            s1 = keep.tile([P, 8], F32, name="s1_%d" % br)
+            nc.vector.tensor_reduce(
+                out=s1[:], in_=s2[:].rearrange("p (mb i) j -> p mb (i j)", i=2), axis=AX.X, op=ALU.add
+            )
+            nc.scalar.mul(
+                out_view[:, :, :, 0:1], s1[:].rearrange("p (m b o) -> p m b o", m=4, o=1), 1.0 / 36.0
+            )
+            dram = (out_0, out_1)[br].rearrange("b (p t) f -> p b (t f)", t=4)
+            nc.sync.dma_start(out=dram, in_=res[br][:].rearrange("p b t f -> p b (t f)"))
+
+        transposes(0)
+        w_out(0)
+        x_regroup(0, "v")
+        x_regroup(0, "s")
+        bn_prepare()
+        for i in range(8):
+            if i < 7:
+                transposes(i + 1)
+                w_out(i + 1)
+            w_quant(i)
+            x_quant(i)
+            if i < 7:
+                x_regroup(i + 1, "v")
+                x_regroup(i + 1, "s")
+            if i < 4:
+                for g in range(i):
+                    mx(0, i, g)
+                for m in range(i + 1):
+                    mx(0, m, i)
+                if i == 3:
+                    for m in range(4):
+                        y_out(0, m)
+            else:
+                for g in range(4):
+                    mx(0, i, g)
+                for m in range(4):
+                    mx(1, m, i - 4)
+                y_out(0, i)
+                pool(0, i - 4)
+        for m in range(4, 8):
+            y_out(1, m - 4)
+            pool(0, m)
+            pool(1, m - 4)
+            for g in range(4):
+                mx(1, m, g)
+        for m in range(8):
+            if m < 4:
+                y_out(1, m + 4)
+                pool(1, m + 4)
+            for g in range(4):
+                mx(2, m, g)
+            y_out(2, m)
+            pool(2, m)
+            if m == 3:
+                finish(0)
+        finish(1)

@@ -17,9 +17,237 @@ AX = mybir.AxisListType
 P = 128
 EPS = 1e-5
 NPOS = 576
-PIN = False
+PIN = True
 CS = (192, 128)
-WXV = (4, 5, 6, 7)
+ORDER = (
+    ("T", 0, 0),
+    ("T", 0, 1),
+    ("WX", 0, 0, "s"),
+    ("WX", 0, 1, "s"),
+    ("XR", 0, "v"),
+    ("XR", 0, "s"),
+    ("WQ", 0),
+    ("T", 1, 0),
+    ("T", 1, 1),
+    ("XQ", 0),
+    ("WX", 1, 0, "s"),
+    ("WX", 1, 1, "s"),
+    ("XR", 1, "v"),
+    ("M", 0, 0, 0),
+    ("XR", 1, "s"),
+    ("WQ", 1),
+    ("T", 2, 0),
+    ("T", 2, 1),
+    ("XQ", 1),
+    ("WX", 2, 0, "s"),
+    ("M", 0, 1, 0),
+    ("WX", 2, 1, "s"),
+    ("XR", 2, "v"),
+    ("M", 0, 0, 1),
+    ("XR", 2, "s"),
+    ("M", 0, 1, 1),
+    ("WQ", 2),
+    ("T", 3, 0),
+    ("T", 3, 1),
+    ("XQ", 2),
+    ("WX", 3, 0, "s"),
+    ("M", 0, 2, 0),
+    ("M", 0, 2, 1),
+    ("WX", 3, 1, "s"),
+    ("XR", 3, "v"),
+    ("M", 0, 0, 2),
+    ("XR", 3, "s"),
+    ("M", 0, 1, 2),
+    ("M", 0, 2, 2),
+    ("WQ", 3),
+    ("BN1",),
+    ("BNS",),
+    ("T", 4, 0),
+    ("XQ", 3),
+    ("BN2",),
+    ("T", 4, 1),
+    ("WX", 4, 0, "s"),
+    ("M", 0, 3, 0),
+    ("M", 0, 3, 1),
+    ("WX", 4, 1, "s"),
+    ("XR", 4, "v"),
+    ("M", 0, 3, 2),
+    ("M", 0, 0, 3),
+    ("XR", 4, "s"),
+    ("M", 0, 1, 3),
+    ("WQ", 4),
+    ("M", 0, 2, 3),
+    ("YX", 0, 0),
+    ("M", 0, 3, 3),
+    ("T", 5, 0),
+    ("XQ", 4),
+    ("YX", 0, 1),
+    ("T", 5, 1),
+    ("PL", 0, 0),
+    ("M", 0, 4, 0),
+    ("WX", 5, 0, "s"),
+    ("M", 0, 4, 1),
+    ("XR", 5, "v"),
+    ("M", 0, 4, 2),
+    ("WX", 5, 1, "s"),
+    ("M", 0, 4, 3),
+    ("T", 6, 0),
+    ("XR", 5, "s"),
+    ("WQ", 5),
+    ("T", 6, 1),
+    ("WX", 6, 0, "s"),
+    ("XQ", 5),
+    ("WX", 6, 1, "s"),
+    ("M", 0, 5, 0),
+    ("XR", 6, "v"),
+    ("M", 0, 5, 1),
+    ("XR", 6, "s"),
+    ("M", 0, 5, 2),
+    ("M", 0, 5, 3),
+    ("YX", 0, 2),
+    ("M", 1, 0, 0),
+    ("WQ", 6),
+    ("M", 1, 1, 0),
+    ("YX", 0, 3),
+    ("M", 1, 2, 0),
+    ("XQ", 6),
+    ("T", 7, 0),
+    ("XR", 7, "s"),
+    ("T", 7, 1),
+    ("XR", 7, "v"),
+    ("M", 0, 6, 0),
+    ("WX", 7, 0, "s"),
+    ("M", 0, 6, 1),
+    ("M", 0, 6, 2),
+    ("XQ", 7),
+    ("WX", 7, 1, "s"),
+    ("M", 0, 6, 3),
+    ("M", 1, 0, 1),
+    ("YX", 0, 4),
+    ("PL", 0, 1),
+    ("M", 1, 1, 1),
+    ("M", 1, 2, 1),
+    ("WQ", 7),
+    ("YX", 0, 5),
+    ("M", 1, 0, 2),
+    ("M", 1, 1, 2),
+    ("PL", 0, 2),
+    ("M", 1, 2, 2),
+    ("YX", 0, 6),
+    ("M", 0, 7, 0),
+    ("PL", 0, 3),
+    ("M", 0, 7, 1),
+    ("M", 0, 7, 2),
+    ("PL", 0, 4),
+    ("M", 0, 7, 3),
+    ("M", 1, 0, 3),
+    ("PL", 0, 5),
+    ("YX", 0, 7),
+    ("M", 1, 1, 3),
+    ("M", 1, 2, 3),
+    ("PL", 0, 6),
+    ("M", 1, 3, 0),
+    ("YX", 1, 0),
+    ("M", 1, 3, 1),
+    ("PL", 0, 7),
+    ("M", 1, 3, 2),
+    ("YX", 1, 1),
+    ("M", 1, 3, 3),
+    ("PL", 1, 0),
+    ("M", 2, 0, 0),
+    ("M", 2, 0, 1),
+    ("M", 2, 0, 2),
+    ("M", 2, 0, 3),
+    ("YX", 1, 2),
+    ("M", 2, 1, 0),
+    ("M", 2, 1, 1),
+    ("M", 2, 1, 2),
+    ("M", 2, 1, 3),
+    ("PL", 1, 1),
+    ("M", 2, 2, 0),
+    ("M", 2, 2, 1),
+    ("M", 2, 2, 2),
+    ("M", 2, 2, 3),
+    ("YX", 1, 3),
+    ("M", 2, 3, 0),
+    ("M", 2, 3, 1),
+    ("M", 2, 3, 2),
+    ("PL", 1, 2),
+    ("M", 2, 3, 3),
+    ("M", 1, 4, 0),
+    ("M", 1, 4, 1),
+    ("YX", 2, 0),
+    ("PL", 1, 3),
+    ("M", 1, 4, 2),
+    ("YX", 2, 1),
+    ("M", 1, 4, 3),
+    ("YX", 2, 2),
+    ("PL", 2, 0),
+    ("YX", 2, 3),
+    ("M", 1, 5, 0),
+    ("YX", 1, 4),
+    ("PL", 2, 1),
+    ("M", 1, 5, 1),
+    ("PL", 2, 2),
+    ("M", 1, 5, 2),
+    ("PL", 2, 3),
+    ("M", 1, 5, 3),
+    ("F", "2r", 0, 4),
+    ("M", 1, 6, 0),
+    ("F", "6", 0, 4),
+    ("M", 1, 6, 1),
+    ("PL", 1, 4),
+    ("YX", 1, 5),
+    ("M", 1, 6, 2),
+    ("M", 1, 6, 3),
+    ("F", "3r", 0, 4),
+    ("M", 1, 7, 0),
+    ("F", "2s", 0, 4),
+    ("F", "1r", 0, 4),
+    ("YX", 1, 6),
+    ("M", 1, 7, 1),
+    ("PL", 1, 5),
+    ("M", 1, 7, 2),
+    ("M", 1, 7, 3),
+    ("F", "3s", 0, 4),
+    ("F", "1s", 0, 4),
+    ("PL", 1, 6),
+    ("M", 2, 4, 0),
+    ("M", 2, 4, 1),
+    ("M", 2, 4, 2),
+    ("YX", 1, 7),
+    ("M", 2, 4, 3),
+    ("M", 2, 5, 0),
+    ("M", 2, 5, 1),
+    ("M", 2, 5, 2),
+    ("M", 2, 5, 3),
+    ("M", 2, 6, 0),
+    ("M", 2, 6, 1),
+    ("M", 2, 6, 2),
+    ("YX", 2, 4),
+    ("M", 2, 6, 3),
+    ("M", 2, 7, 0),
+    ("M", 2, 7, 1),
+    ("PL", 1, 7),
+    ("M", 2, 7, 2),
+    ("YX", 2, 5),
+    ("M", 2, 7, 3),
+    ("YX", 2, 6),
+    ("PL", 2, 4),
+    ("YX", 2, 7),
+    ("PL", 2, 5),
+    ("ST", 0),
+    ("PL", 2, 6),
+    ("PL", 2, 7),
+    ("F", "2r", 4, 4),
+    ("F", "6", 4, 4),
+    ("F", "3r", 4, 4),
+    ("F", "2s", 4, 4),
+    ("F", "1r", 4, 4),
+    ("F", "3s", 4, 4),
+    ("F", "1s", 4, 4),
+    ("ST", 1),
+)
 
 
 def tile_guided_cam_module2_pa_kernel(
@@ -46,12 +274,12 @@ def tile_guided_cam_module2_pa_kernel(
             nc.sync.dma_start(out=xt[:], in_=xv[i // 4, i % 4])
             xraw.append(xt)
 
-        bnraw = keep.tile([P, 8, 16], BF16, name="bnraw")
-        for v, vec in enumerate((q_scale, k_scale, q_bias, k_bias, q_mean, k_mean, q_var, k_var)):
-            nc.scalar.dma_start(out=bnraw[:, v, 0:4], in_=vec.rearrange("(p t) -> p t", t=4))
-
         ident = keep.tile([P, P], F32, name="ident")
         make_identity(nc, ident[:])
+
+        bnraw = keep.tile([P, 8, 16], BF16, name="bnraw")
+        for v, vec in enumerate((q_var, k_var, q_scale, k_scale, q_mean, k_mean, q_bias, k_bias)):
+            nc.gpsimd.dma_start(out=bnraw[:, v, 0:4], in_=vec.rearrange("(p t) -> p t", t=4))
 
         warm = keep.tile([P, 2], F32, name="warm")
         nc.vector.memset(warm[:, 0:1], 1.0)
@@ -67,22 +295,27 @@ def tile_guided_cam_module2_pa_kernel(
         a16 = keep.tile([P, 8], F32, name="a16")
         c16 = keep.tile([P, 8], F32, name="c16")
 
-        def bn_prepare():
-            bn32 = keep.tile([P, 8, 4], F32, name="bn32")
+        bn32 = keep.tile([P, 8, 4], F32, name="bn32")
+        bnflat = bn32[:].rearrange("p v t -> p (v t)")
+        sd = keep.tile([P, 8], F32, name="sd")
+        rstd = keep.tile([P, 8], F32, name="rstd")
+        ma = keep.tile([P, 8], F32, name="ma")
+
+        def bn_first():
             nc.vector.tensor_copy(out=bn32[:], in_=bnraw[:, :, 0:4])
-            flat = bn32[:].rearrange("p v t -> p (v t)")
-            sd = keep.tile([P, 8], F32, name="sd")
-            nc.vector.tensor_scalar_add(out=sd[:], in0=flat[:, 24:32], scalar1=EPS)
+            nc.vector.tensor_scalar_add(out=sd[:], in0=bnflat[:, 0:8], scalar1=EPS)
+
+        def bn_sqrt():
             nc.scalar.sqrt(sd[:], sd[:])
-            rstd = keep.tile([P, 8], F32, name="rstd")
+
+        def bn_last():
             nc.vector.reciprocal(out=rstd[:], in_=sd[:])
             nc.vector.scalar_tensor_tensor(
-                out=a16[:], in0=flat[:, 0:8], scalar=1.0 / 16.0, in1=rstd[:], op0=ALU.mult, op1=ALU.mult
+                out=a16[:], in0=bnflat[:, 8:16], scalar=1.0 / 16.0, in1=rstd[:], op0=ALU.mult, op1=ALU.mult
             )
-            ma = keep.tile([P, 8], F32, name="ma")
-            nc.vector.tensor_mul(out=ma[:], in0=flat[:, 16:24], in1=a16[:])
+            nc.vector.tensor_mul(out=ma[:], in0=bnflat[:, 16:24], in1=a16[:])
             nc.vector.scalar_tensor_tensor(
-                out=c16[:], in0=flat[:, 8:16], scalar=1.0 / 16.0, in1=ma[:], op0=ALU.mult, op1=ALU.subtract
+                out=c16[:], in0=bnflat[:, 24:32], scalar=1.0 / 16.0, in1=ma[:], op0=ALU.mult, op1=ALU.subtract
             )
 
         tps = {}
@@ -90,26 +323,24 @@ def tile_guided_cam_module2_pa_kernel(
         xgs = {}
         ys = {}
 
-        def transposes(m):
+        def transposes(m, h):
             w32 = wraw[m][:].bitcast(F32)
-            for h in range(2):
-                tp = psum.tile([P, 4, P], F32, name="tp%d_%d" % (m, h), tag="bank")
-                for j in range(4):
-                    blk = 4 * h + j
-                    nc.tensor.transpose(tp[:, j, :], w32[:, P * blk : P * (blk + 1)], ident[:])
-                tps[(m, h)] = tp
+            tp = psum.tile([P, 4, P], F32, name="tp%d_%d" % (m, h), tag="bank")
+            for j in range(4):
+                blk = 4 * h + j
+                nc.tensor.transpose(tp[:, j, :], w32[:, P * blk : P * (blk + 1)], ident[:])
+            tps[(m, h)] = tp
 
-        def w_out(m):
-            wg = wgrp_pool.tile([P, 2048], BF16, name="wg%d" % m, tag="wg", align_bytes=64)
-            wgs[m] = wg
-            wg32 = wg[:].bitcast(F32).rearrange("p (g c u) -> p g c u", g=4, c=P, u=2)
-            for h in range(2):
-                src = tps[(m, h)][:].rearrange("p (g u) c -> p g c u", u=2)
-                dst = wg32[:, 2 * h : 2 * h + 2, :, :]
-                if h == 1 and m in WXV:
-                    nc.vector.tensor_copy(out=dst, in_=src)
-                else:
-                    nc.scalar.copy(out=dst, in_=src)
+        def w_out(m, h, engine):
+            if m not in wgs:
+                wgs[m] = wgrp_pool.tile([P, 2048], BF16, name="wg%d" % m, tag="wg", align_bytes=64)
+            wg32 = wgs[m][:].bitcast(F32).rearrange("p (g c u) -> p g c u", g=4, c=P, u=2)
+            src = tps[(m, h)][:].rearrange("p (g u) c -> p g c u", u=2)
+            dst = wg32[:, 2 * h : 2 * h + 2, :, :]
+            if engine == "v":
+                nc.vector.tensor_copy(out=dst, in_=src)
+            else:
+                nc.scalar.copy(out=dst, in_=src)
 
         def w_quant(m):
             nc.vector.quantize_mx(out=wc[m][:].bitcast(FP8X4), scales=ws[m][:], in_=wgs[m][:])
@@ -178,84 +409,75 @@ def tile_guided_cam_module2_pa_kernel(
                 dst = l6[:, m, :, 30:36]
             nc.vector.tensor_reduce(out=dst, in_=src, axis=AX.XY, op=ALU.add)
 
-        def finish(br):
-            m0 = 4 * br
-            part = l6[:, m0 : m0 + 4, :, :]
-            out_view = res[br][:].rearrange("p b t f -> p t b f")
-            nc.scalar.copy(out=out_view[:, :, :, 14:50], in_=part)
-            s3 = keep.tile([P, 24, 3], F32, name="s3_%d" % br)
-            nc.vector.tensor_reduce(
-                out=s3[:],
-                in_=part.rearrange("p m b (i di j dj) -> p (m b i) j di dj", i=3, di=2, j=3, dj=2),
-                axis=AX.XY,
-                op=ALU.add,
-            )
-            nc.scalar.mul(
-                out_view[:, :, :, 5:14], s3[:].rearrange("p (m b i) j -> p m b (i j)", m=4, b=2), 0.25
-            )
-            s2 = keep.tile([P, 16, 2], F32, name="s2_%d" % br)
-            nc.vector.tensor_reduce(
-                out=s2[:],
-                in_=part.rearrange("p m b (i di j dj) -> p (m b i) j di dj", i=2, di=3, j=2, dj=3),
-                axis=AX.XY,
-                op=ALU.add,
-            )
-            nc.scalar.mul(
-                out_view[:, :, :, 1:5], s2[:].rearrange("p (m b i) j -> p m b (i j)", m=4, b=2), 1.0 / 9.0
-            )
-            s1 = keep.tile([P, 8], F32, name="s1_%d" % br)
-            nc.vector.tensor_reduce(
-                out=s1[:], in_=s2[:].rearrange("p (mb i) j -> p mb (i j)", i=2), axis=AX.X, op=ALU.add
-            )
-            nc.scalar.mul(
-                out_view[:, :, :, 0:1], s1[:].rearrange("p (m b o) -> p m b o", m=4, o=1), 1.0 / 36.0
-            )
+        sums = {}
+
+        def fin(step, m0, n):
+            br, t0 = m0 // 4, m0 % 4
+            part = l6[:, m0 : m0 + n, :, :]
+            out_view = res[br][:].rearrange("p b t f -> p t b f")[:, t0 : t0 + n, :, :]
+            if step == "6":
+                nc.scalar.copy(out=out_view[:, :, :, 14:50], in_=part)
+            elif step == "3r":
+                sums[(3, m0)] = keep.tile([P, 6 * n, 3], F32, name="s3_%d" % m0)
+                nc.vector.tensor_reduce(
+                    out=sums[(3, m0)][:],
+                    in_=part.rearrange("p m b (i di j dj) -> p (m b i) j di dj", i=3, di=2, j=3, dj=2),
+                    axis=AX.XY,
+                    op=ALU.add,
+                )
+            elif step == "3s":
+                nc.scalar.mul(
+                    out_view[:, :, :, 5:14],
+                    sums[(3, m0)][:].rearrange("p (m b i) j -> p m b (i j)", m=n, b=2),
+                    0.25,
+                )
+            elif step == "2r":
+                sums[(2, m0)] = keep.tile([P, 4 * n, 2], F32, name="s2_%d" % m0)
+                nc.vector.tensor_reduce(
+                    out=sums[(2, m0)][:],
+                    in_=part.rearrange("p m b (i di j dj) -> p (m b i) j di dj", i=2, di=3, j=2, dj=3),
+                    axis=AX.XY,
+                    op=ALU.add,
+                )
+            elif step == "2s":
+                nc.scalar.mul(
+                    out_view[:, :, :, 1:5],
+                    sums[(2, m0)][:].rearrange("p (m b i) j -> p m b (i j)", m=n, b=2),
+                    1.0 / 9.0,
+                )
+            elif step == "1r":
+                sums[(1, m0)] = keep.tile([P, 2 * n], F32, name="s1_%d" % m0)
+                nc.vector.tensor_reduce(
+                    out=sums[(1, m0)][:],
+                    in_=sums[(2, m0)][:].rearrange("p (mb i) j -> p mb (i j)", i=2),
+                    axis=AX.X,
+                    op=ALU.add,
+                )
+            else:
+                nc.scalar.mul(
+                    out_view[:, :, :, 0:1],
+                    sums[(1, m0)][:].rearrange("p (m b o) -> p m b o", m=n, o=1),
+                    1.0 / 36.0,
+                )
+
+        def store(br):
             dram = (out_0, out_1)[br].rearrange("b (p t) f -> p b (t f)", t=4)
             nc.sync.dma_start(out=dram, in_=res[br][:].rearrange("p b t f -> p b (t f)"))
 
-        transposes(0)
-        w_out(0)
-        x_regroup(0, "v")
-        x_regroup(0, "s")
-        bn_prepare()
-        for i in range(8):
-            if i < 7:
-                transposes(i + 1)
-                w_out(i + 1)
-            w_quant(i)
-            x_quant(i)
-            if i < 7:
-                x_regroup(i + 1, "v")
-                x_regroup(i + 1, "s")
-            if i < 4:
-                for g in range(i):
-                    mx(0, i, g)
-                for m in range(i + 1):
-                    mx(0, m, i)
-                if i == 3:
-                    for m in range(4):
-                        y_out(0, m)
-            else:
-                for g in range(4):
-                    mx(0, i, g)
-                for m in range(4):
-                    mx(1, m, i - 4)
-                y_out(0, i)
-                pool(0, i - 4)
-        for m in range(4, 8):
-            y_out(1, m - 4)
-            pool(0, m)
-            pool(1, m - 4)
-            for g in range(4):
-                mx(1, m, g)
-        for m in range(8):
-            if m < 4:
-                y_out(1, m + 4)
-                pool(1, m + 4)
-            for g in range(4):
-                mx(2, m, g)
-            y_out(2, m)
-            pool(2, m)
-            if m == 3:
-                finish(0)
-        finish(1)
+        calls = {
+            "T": transposes,
+            "WX": w_out,
+            "WQ": w_quant,
+            "XR": x_regroup,
+            "XQ": x_quant,
+            "M": mx,
+            "YX": y_out,
+            "PL": pool,
+            "F": fin,
+            "ST": store,
+            "BN1": bn_first,
+            "BNS": bn_sqrt,
+            "BN2": bn_last,
+        }
+        for step in ORDER:
+            calls[step[0]](*step[1:])

@@ -20,6 +20,8 @@ NPOS = 576
 PIN = True
 CS = (192, 128)
 ORDER = (
+    ("BN1",),
+    ("BNS",),
     ("T", 0, 0),
     ("T", 0, 1),
     ("WX", 0, 0, "s"),
@@ -30,6 +32,7 @@ ORDER = (
     ("T", 1, 0),
     ("T", 1, 1),
     ("XQ", 0),
+    ("BN2",),
     ("WX", 1, 0, "s"),
     ("WX", 1, 1, "s"),
     ("XR", 1, "v"),
@@ -60,11 +63,8 @@ ORDER = (
     ("M", 0, 1, 2),
     ("M", 0, 2, 2),
     ("WQ", 3),
-    ("BN1",),
-    ("BNS",),
     ("T", 4, 0),
     ("XQ", 3),
-    ("BN2",),
     ("T", 4, 1),
     ("WX", 4, 0, "s"),
     ("M", 0, 3, 0),
@@ -262,10 +262,16 @@ def tile_guided_cam_module2_pa_kernel(
         if PIN:
             ctx.enter_context(tc.manual_schedule())
 
+        warm = keep.tile([P, 2], F32, name="warm")
+        nc.vector.memset(warm[:, 0:1], 1.0)
+        nc.scalar.sqrt(warm[:, 1:2], warm[:, 0:1])
+
         xv = x.rearrange("b (g u p e) h w -> b g p u (e h w)", g=4, u=2, p=P, e=2)
         wv = [wq.rearrange("(p t) k -> p t k", t=4), wk.rearrange("(p t) k -> p t k", t=4)]
         wraw = []
         xraw = []
+        bnraw = keep.tile([P, 8, 16], BF16, name="bnraw")
+        bnvecs = (q_var, k_var, q_scale, k_scale, q_mean, k_mean, q_bias, k_bias)
         for i in range(8):
             wt = keep.tile([P, 2048], BF16, name="wraw%d" % i)
             nc.sync.dma_start(out=wt[:], in_=wv[i // 4][:, i % 4, :])
@@ -273,17 +279,12 @@ def tile_guided_cam_module2_pa_kernel(
             xt = keep.tile([P, 2, 2 * NPOS], BF16, name="xraw%d" % i)
             nc.sync.dma_start(out=xt[:], in_=xv[i // 4, i % 4])
             xraw.append(xt)
+            if i in (0, 2):
+                for v in range(2 * i, 2 * i + 4):
+                    nc.scalar.dma_start(out=bnraw[:, v, 0:4], in_=bnvecs[v].rearrange("(p t) -> p t", t=4))
 
         ident = keep.tile([P, P], F32, name="ident")
         make_identity(nc, ident[:])
-
-        bnraw = keep.tile([P, 8, 16], BF16, name="bnraw")
-        for v, vec in enumerate((q_var, k_var, q_scale, k_scale, q_mean, k_mean, q_bias, k_bias)):
-            nc.gpsimd.dma_start(out=bnraw[:, v, 0:4], in_=vec.rearrange("(p t) -> p t", t=4))
-
-        warm = keep.tile([P, 2], F32, name="warm")
-        nc.vector.memset(warm[:, 0:1], 1.0)
-        nc.scalar.sqrt(warm[:, 1:2], warm[:, 0:1])
 
         wc = [keep.tile([P, 512], U32, name="wc%d" % m, align_bytes=64) for m in range(8)]
         ws = [keep.tile([P, 512], U8, name="ws%d" % m, align_bytes=64) for m in range(8)]
@@ -295,15 +296,15 @@ def tile_guided_cam_module2_pa_kernel(
         a16 = keep.tile([P, 8], F32, name="a16")
         c16 = keep.tile([P, 8], F32, name="c16")
 
-        bn32 = keep.tile([P, 8, 4], F32, name="bn32")
-        bnflat = bn32[:].rearrange("p v t -> p (v t)")
         sd = keep.tile([P, 8], F32, name="sd")
         rstd = keep.tile([P, 8], F32, name="rstd")
         ma = keep.tile([P, 8], F32, name="ma")
 
+        def by_branch(tile8):
+            return tile8[:].rearrange("p (r t) -> p r t", r=2)
+
         def bn_first():
-            nc.vector.tensor_copy(out=bn32[:], in_=bnraw[:, :, 0:4])
-            nc.vector.tensor_scalar_add(out=sd[:], in0=bnflat[:, 0:8], scalar1=EPS)
+            nc.vector.tensor_scalar_add(out=by_branch(sd), in0=bnraw[:, 0:2, 0:4], scalar1=EPS)
 
         def bn_sqrt():
             nc.scalar.sqrt(sd[:], sd[:])
@@ -311,11 +312,13 @@ def tile_guided_cam_module2_pa_kernel(
         def bn_last():
             nc.vector.reciprocal(out=rstd[:], in_=sd[:])
             nc.vector.scalar_tensor_tensor(
-                out=a16[:], in0=bnflat[:, 8:16], scalar=1.0 / 16.0, in1=rstd[:], op0=ALU.mult, op1=ALU.mult
+                out=by_branch(a16), in0=bnraw[:, 2:4, 0:4], scalar=1.0 / 16.0, in1=by_branch(rstd),
+                op0=ALU.mult, op1=ALU.mult,
             )
-            nc.vector.tensor_mul(out=ma[:], in0=bnflat[:, 16:24], in1=a16[:])
+            nc.vector.tensor_mul(out=by_branch(ma), in0=bnraw[:, 4:6, 0:4], in1=by_branch(a16))
             nc.vector.scalar_tensor_tensor(
-                out=c16[:], in0=bnflat[:, 24:32], scalar=1.0 / 16.0, in1=ma[:], op0=ALU.mult, op1=ALU.subtract
+                out=by_branch(c16), in0=bnraw[:, 6:8, 0:4], scalar=1.0 / 16.0, in1=by_branch(ma),
+                op0=ALU.mult, op1=ALU.subtract,
             )
 
         tps = {}

@@ -10,6 +10,7 @@ BF16 = mybir.dt.bfloat16
 F32 = mybir.dt.float32
 U32 = mybir.dt.uint32
 U8 = mybir.dt.uint8
+I32 = mybir.dt.int32
 ALU = mybir.AluOpType
 ACT = mybir.ActivationFunctionType
 AX = mybir.AxisListType
@@ -17,237 +18,12 @@ AX = mybir.AxisListType
 P = 128
 EPS = 1e-5
 NPOS = 576
+LAST_POOL = (16, 24)
 PIN = True
-CS = (192, 128)
-ORDER = (
-    ("BN1",),
-    ("BNS",),
-    ("T", 0, 0),
-    ("T", 0, 1),
-    ("WX", 0, 0, "s"),
-    ("WX", 0, 1, "s"),
-    ("XR", 0, "v"),
-    ("XR", 0, "s"),
-    ("WQ", 0),
-    ("T", 1, 0),
-    ("T", 1, 1),
-    ("XQ", 0),
-    ("BN2",),
-    ("WX", 1, 0, "s"),
-    ("WX", 1, 1, "s"),
-    ("XR", 1, "v"),
-    ("M", 0, 0, 0),
-    ("XR", 1, "s"),
-    ("WQ", 1),
-    ("T", 2, 0),
-    ("T", 2, 1),
-    ("XQ", 1),
-    ("WX", 2, 0, "s"),
-    ("M", 0, 1, 0),
-    ("WX", 2, 1, "s"),
-    ("XR", 2, "v"),
-    ("M", 0, 0, 1),
-    ("XR", 2, "s"),
-    ("M", 0, 1, 1),
-    ("WQ", 2),
-    ("T", 3, 0),
-    ("T", 3, 1),
-    ("XQ", 2),
-    ("WX", 3, 0, "s"),
-    ("M", 0, 2, 0),
-    ("M", 0, 2, 1),
-    ("WX", 3, 1, "s"),
-    ("XR", 3, "v"),
-    ("M", 0, 0, 2),
-    ("XR", 3, "s"),
-    ("M", 0, 1, 2),
-    ("M", 0, 2, 2),
-    ("WQ", 3),
-    ("T", 4, 0),
-    ("XQ", 3),
-    ("T", 4, 1),
-    ("WX", 4, 0, "s"),
-    ("M", 0, 3, 0),
-    ("M", 0, 3, 1),
-    ("WX", 4, 1, "s"),
-    ("XR", 4, "v"),
-    ("M", 0, 3, 2),
-    ("M", 0, 0, 3),
-    ("XR", 4, "s"),
-    ("M", 0, 1, 3),
-    ("WQ", 4),
-    ("M", 0, 2, 3),
-    ("YX", 0, 0),
-    ("M", 0, 3, 3),
-    ("T", 5, 0),
-    ("XQ", 4),
-    ("YX", 0, 1),
-    ("T", 5, 1),
-    ("PL", 0, 0),
-    ("M", 0, 4, 0),
-    ("WX", 5, 0, "s"),
-    ("M", 0, 4, 1),
-    ("XR", 5, "v"),
-    ("M", 0, 4, 2),
-    ("WX", 5, 1, "s"),
-    ("M", 0, 4, 3),
-    ("T", 6, 0),
-    ("XR", 5, "s"),
-    ("WQ", 5),
-    ("T", 6, 1),
-    ("WX", 6, 0, "s"),
-    ("XQ", 5),
-    ("WX", 6, 1, "s"),
-    ("M", 0, 5, 0),
-    ("XR", 6, "v"),
-    ("M", 0, 5, 1),
-    ("XR", 6, "s"),
-    ("M", 0, 5, 2),
-    ("M", 0, 5, 3),
-    ("YX", 0, 2),
-    ("M", 1, 0, 0),
-    ("WQ", 6),
-    ("M", 1, 1, 0),
-    ("YX", 0, 3),
-    ("M", 1, 2, 0),
-    ("XQ", 6),
-    ("T", 7, 0),
-    ("XR", 7, "s"),
-    ("T", 7, 1),
-    ("XR", 7, "v"),
-    ("M", 0, 6, 0),
-    ("WX", 7, 0, "s"),
-    ("M", 0, 6, 1),
-    ("M", 0, 6, 2),
-    ("XQ", 7),
-    ("WX", 7, 1, "s"),
-    ("M", 0, 6, 3),
-    ("M", 1, 0, 1),
-    ("YX", 0, 4),
-    ("PL", 0, 1),
-    ("M", 1, 1, 1),
-    ("M", 1, 2, 1),
-    ("WQ", 7),
-    ("YX", 0, 5),
-    ("M", 1, 0, 2),
-    ("M", 1, 1, 2),
-    ("PL", 0, 2),
-    ("M", 1, 2, 2),
-    ("YX", 0, 6),
-    ("M", 0, 7, 0),
-    ("PL", 0, 3),
-    ("M", 0, 7, 1),
-    ("M", 0, 7, 2),
-    ("PL", 0, 4),
-    ("M", 0, 7, 3),
-    ("M", 1, 0, 3),
-    ("PL", 0, 5),
-    ("YX", 0, 7),
-    ("M", 1, 1, 3),
-    ("M", 1, 2, 3),
-    ("PL", 0, 6),
-    ("M", 1, 3, 0),
-    ("YX", 1, 0),
-    ("M", 1, 3, 1),
-    ("PL", 0, 7),
-    ("M", 1, 3, 2),
-    ("YX", 1, 1),
-    ("M", 1, 3, 3),
-    ("PL", 1, 0),
-    ("M", 2, 0, 0),
-    ("M", 2, 0, 1),
-    ("M", 2, 0, 2),
-    ("M", 2, 0, 3),
-    ("YX", 1, 2),
-    ("M", 2, 1, 0),
-    ("M", 2, 1, 1),
-    ("M", 2, 1, 2),
-    ("M", 2, 1, 3),
-    ("PL", 1, 1),
-    ("M", 2, 2, 0),
-    ("M", 2, 2, 1),
-    ("M", 2, 2, 2),
-    ("M", 2, 2, 3),
-    ("YX", 1, 3),
-    ("M", 2, 3, 0),
-    ("M", 2, 3, 1),
-    ("M", 2, 3, 2),
-    ("PL", 1, 2),
-    ("M", 2, 3, 3),
-    ("M", 1, 4, 0),
-    ("M", 1, 4, 1),
-    ("YX", 2, 0),
-    ("PL", 1, 3),
-    ("M", 1, 4, 2),
-    ("YX", 2, 1),
-    ("M", 1, 4, 3),
-    ("YX", 2, 2),
-    ("PL", 2, 0),
-    ("YX", 2, 3),
-    ("M", 1, 5, 0),
-    ("YX", 1, 4),
-    ("PL", 2, 1),
-    ("M", 1, 5, 1),
-    ("PL", 2, 2),
-    ("M", 1, 5, 2),
-    ("PL", 2, 3),
-    ("M", 1, 5, 3),
-    ("F", "2r", 0, 4),
-    ("M", 1, 6, 0),
-    ("F", "6", 0, 4),
-    ("M", 1, 6, 1),
-    ("PL", 1, 4),
-    ("YX", 1, 5),
-    ("M", 1, 6, 2),
-    ("M", 1, 6, 3),
-    ("F", "3r", 0, 4),
-    ("M", 1, 7, 0),
-    ("F", "2s", 0, 4),
-    ("F", "1r", 0, 4),
-    ("YX", 1, 6),
-    ("M", 1, 7, 1),
-    ("PL", 1, 5),
-    ("M", 1, 7, 2),
-    ("M", 1, 7, 3),
-    ("F", "3s", 0, 4),
-    ("F", "1s", 0, 4),
-    ("PL", 1, 6),
-    ("M", 2, 4, 0),
-    ("M", 2, 4, 1),
-    ("M", 2, 4, 2),
-    ("YX", 1, 7),
-    ("M", 2, 4, 3),
-    ("M", 2, 5, 0),
-    ("M", 2, 5, 1),
-    ("M", 2, 5, 2),
-    ("M", 2, 5, 3),
-    ("M", 2, 6, 0),
-    ("M", 2, 6, 1),
-    ("M", 2, 6, 2),
-    ("YX", 2, 4),
-    ("M", 2, 6, 3),
-    ("M", 2, 7, 0),
-    ("M", 2, 7, 1),
-    ("PL", 1, 7),
-    ("M", 2, 7, 2),
-    ("YX", 2, 5),
-    ("M", 2, 7, 3),
-    ("YX", 2, 6),
-    ("PL", 2, 4),
-    ("YX", 2, 7),
-    ("PL", 2, 5),
-    ("ST", 0),
-    ("PL", 2, 6),
-    ("PL", 2, 7),
-    ("F", "2r", 4, 4),
-    ("F", "6", 4, 4),
-    ("F", "3r", 4, 4),
-    ("F", "2s", 4, 4),
-    ("F", "1r", 4, 4),
-    ("F", "3s", 4, 4),
-    ("F", "1s", 4, 4),
-    ("ST", 1),
-)
+CS = (224, 128)
+KB = 3
+EXITS = {4: 2, 5: 1, 6: 1}
+POOLS = {5: 1, 6: 1}
 
 
 def tile_guided_cam_module2_pa_kernel(
@@ -270,7 +46,8 @@ def tile_guided_cam_module2_pa_kernel(
         wv = [wq.rearrange("(p t) k -> p t k", t=4), wk.rearrange("(p t) k -> p t k", t=4)]
         wraw = []
         xraw = []
-        bnraw = keep.tile([P, 8, 16], BF16, name="bnraw")
+        bnrows = keep.tile([P, 512], BF16, name="bnrows")
+        nc.vector.memset(bnrows[:].bitcast(I32), 0)
         bnvecs = (q_var, k_var, q_scale, k_scale, q_mean, k_mean, q_bias, k_bias)
         for i in range(8):
             wt = keep.tile([P, 2048], BF16, name="wraw%d" % i)
@@ -281,7 +58,7 @@ def tile_guided_cam_module2_pa_kernel(
             xraw.append(xt)
             if i in (0, 2):
                 for v in range(2 * i, 2 * i + 4):
-                    nc.scalar.dma_start(out=bnraw[:, v, 0:4], in_=bnvecs[v].rearrange("(p t) -> p t", t=4))
+                    nc.sync.dma_start(out=bnrows[v : v + 1, :], in_=bnvecs[v].rearrange("(o c) -> o c", o=1))
 
         ident = keep.tile([P, P], F32, name="ident")
         make_identity(nc, ident[:])
@@ -300,11 +77,22 @@ def tile_guided_cam_module2_pa_kernel(
         rstd = keep.tile([P, 8], F32, name="rstd")
         ma = keep.tile([P, 8], F32, name="ma")
 
-        def by_branch(tile8):
-            return tile8[:].rearrange("p (r t) -> p r t", r=2)
+        bnp = keep.tile([P, 8, 4], F32, name="bnp")
+        bnflat = bnp[:].rearrange("p r t -> p (r t)")
+        bnbank = {}
+
+        def bn_transposes():
+            bank = psum.tile([P, 2, P], F32, name="bnbank", tag="bank")
+            words = bnrows[:].bitcast(F32).rearrange("p (c j) -> p j c", j=2)
+            for j in range(2):
+                nc.tensor.transpose(bank[:, j, :], words[:, j, :], ident[:])
+            bnbank[0] = bank
 
         def bn_first():
-            nc.vector.tensor_scalar_add(out=by_branch(sd), in0=bnraw[:, 0:2, 0:4], scalar1=EPS)
+            pairs = bnbank[0][:].rearrange("p j r -> p (j r)").bitcast(BF16)
+            pairs = pairs.rearrange("p (j r e) -> p r j e", j=2, e=2)
+            nc.vector.tensor_copy(out=bnp[:].rearrange("p r (j e) -> p r j e", j=2), in_=pairs[:, 0:8, :, :])
+            nc.vector.tensor_scalar_add(out=sd[:], in0=bnflat[:, 0:8], scalar1=EPS)
 
         def bn_sqrt():
             nc.scalar.sqrt(sd[:], sd[:])
@@ -312,13 +100,11 @@ def tile_guided_cam_module2_pa_kernel(
         def bn_last():
             nc.vector.reciprocal(out=rstd[:], in_=sd[:])
             nc.vector.scalar_tensor_tensor(
-                out=by_branch(a16), in0=bnraw[:, 2:4, 0:4], scalar=1.0 / 16.0, in1=by_branch(rstd),
-                op0=ALU.mult, op1=ALU.mult,
+                out=a16[:], in0=bnflat[:, 8:16], scalar=1.0 / 16.0, in1=rstd[:], op0=ALU.mult, op1=ALU.mult
             )
-            nc.vector.tensor_mul(out=by_branch(ma), in0=bnraw[:, 4:6, 0:4], in1=by_branch(a16))
+            nc.vector.tensor_mul(out=ma[:], in0=bnflat[:, 16:24], in1=a16[:])
             nc.vector.scalar_tensor_tensor(
-                out=by_branch(c16), in0=bnraw[:, 6:8, 0:4], scalar=1.0 / 16.0, in1=by_branch(ma),
-                op0=ALU.mult, op1=ALU.subtract,
+                out=c16[:], in0=bnflat[:, 24:32], scalar=1.0 / 16.0, in1=ma[:], op0=ALU.mult, op1=ALU.subtract
             )
 
         tps = {}
@@ -467,20 +253,73 @@ def tile_guided_cam_module2_pa_kernel(
             dram = (out_0, out_1)[br].rearrange("b (p t) f -> p b (t f)", t=4)
             nc.sync.dma_start(out=dram, in_=res[br][:].rearrange("p b t f -> p b (t f)"))
 
-        calls = {
-            "T": transposes,
-            "WX": w_out,
-            "WQ": w_quant,
-            "XR": x_regroup,
-            "XQ": x_quant,
-            "M": mx,
-            "YX": y_out,
-            "PL": pool,
-            "F": fin,
-            "ST": store,
-            "BN1": bn_first,
-            "BNS": bn_sqrt,
-            "BN2": bn_last,
-        }
-        for step in ORDER:
-            calls[step[0]](*step[1:])
+        closing = []
+        count = {"out": 0, "pooled": 0}
+
+        def passes(c, m):
+            for g in range(4):
+                mx(c, m, g)
+            closing.append((c, m))
+
+        def leave(n):
+            for c, m in closing[count["out"] : count["out"] + n]:
+                y_out(c, m)
+            count["out"] = min(count["out"] + n, len(closing))
+
+        def pool_next(n):
+            for c, m in closing[count["pooled"] : min(count["pooled"] + n, count["out"])]:
+                pool(c, m)
+                count["pooled"] = count["pooled"] + 1
+                for br in range(2):
+                    if count["pooled"] == LAST_POOL[br]:
+                        for step in ("6", "3r", "3s", "2r", "2s", "1r", "1s"):
+                            fin(step, 4 * br, 4)
+                        store(br)
+
+        for m in range(2):
+            transposes(m, 0)
+            transposes(m, 1)
+        for i in range(8):
+            w_out(i, 0, "s")
+            w_out(i, 1, "s")
+            x_regroup(i, "s")
+            x_regroup(i, "v")
+            w_quant(i)
+            if i == 2:
+                bn_first()
+                bn_sqrt()
+            x_quant(i)
+            if i == 2:
+                bn_last()
+            leave(EXITS.get(i, 0))
+            pool_next(POOLS.get(i, 0))
+            if i < 4:
+                for g in range(i):
+                    mx(0, i, g)
+                for m in range(i + 1):
+                    mx(0, m, i)
+                if i == 3:
+                    closing.extend([(0, m) for m in range(4)])
+            else:
+                passes(0, i)
+                for g in ((), (0,), (1, 2), (3,))[i - 4]:
+                    for m in range(KB):
+                        mx(1, m, g)
+                if i == 7:
+                    closing.extend([(1, m) for m in range(KB)])
+            if i < 6:
+                transposes(i + 2, 0)
+                transposes(i + 2, 1)
+                if i == 0:
+                    bn_transposes()
+        for m in range(KB, 4):
+            passes(1, m)
+        for m in range(4):
+            passes(2, m)
+        for m in range(4, 8):
+            passes(1, m)
+        for m in range(4, 8):
+            passes(2, m)
+        for n in range(len(closing)):
+            leave(1)
+            pool_next(1)

@@ -19,6 +19,7 @@ P = 128
 EPS = 1e-5
 NPOS = 576
 LAST_POOL = (16, 24)
+WARM = (4, 2, 2, 2)
 PIN = True
 CS = (224, 128)
 KB = 3
@@ -41,6 +42,16 @@ def tile_guided_cam_module2_pa_kernel(
         warm = keep.tile([P, 2], F32, name="warm")
         nc.vector.memset(warm[:, 0:1], 1.0)
         nc.scalar.sqrt(warm[:, 1:2], warm[:, 0:1])
+
+        zeros = keep.tile([P, 512], BF16, name="zeros")
+        nc.vector.memset(zeros[:].bitcast(I32), 0)
+
+        def idle_matmuls(n, label):
+            scratch = psum.tile([P, 512], F32, name="idle%d" % label, tag="bank")
+            for r in range(n):
+                nc.tensor.matmul(out=scratch[:], lhsT=zeros[:, 0:P], rhs=zeros[:], start=True, stop=True)
+
+        idle_matmuls(WARM[0], 0)
 
         xv = x.rearrange("b (g u p e) h w -> b g p u (e h w)", g=4, u=2, p=P, e=2)
         wv = [wq.rearrange("(p t) k -> p t k", t=4), wk.rearrange("(p t) k -> p t k", t=4)]
@@ -279,6 +290,7 @@ def tile_guided_cam_module2_pa_kernel(
         for m in range(2):
             transposes(m, 0)
             transposes(m, 1)
+            idle_matmuls(WARM[m + 1], m + 1)
         for i in range(8):
             w_out(i, 0, "s")
             w_out(i, 1, "s")
@@ -312,6 +324,7 @@ def tile_guided_cam_module2_pa_kernel(
                 transposes(i + 2, 1)
                 if i == 0:
                     bn_transposes()
+                    idle_matmuls(WARM[3], 3)
         for m in range(KB, 4):
             passes(1, m)
         for m in range(4):

@@ -19,9 +19,8 @@ P = 128
 EPS = 1e-5
 NPOS = 576
 LAST_POOL = (16, 24)
-WARM = (4, 2, 2, 2)
 PIN = True
-CS = (224, 128)
+CS = (192, 96)
 KB = 3
 EXITS = {4: 2, 5: 1, 6: 1}
 POOLS = {5: 1, 6: 1}
@@ -42,16 +41,6 @@ def tile_guided_cam_module2_pa_kernel(
         warm = keep.tile([P, 2], F32, name="warm")
         nc.vector.memset(warm[:, 0:1], 1.0)
         nc.scalar.sqrt(warm[:, 1:2], warm[:, 0:1])
-
-        zeros = keep.tile([P, 512], BF16, name="zeros")
-        nc.vector.memset(zeros[:].bitcast(I32), 0)
-
-        def idle_matmuls(n, label):
-            scratch = psum.tile([P, 512], F32, name="idle%d" % label, tag="bank")
-            for r in range(n):
-                nc.tensor.matmul(out=scratch[:], lhsT=zeros[:, 0:P], rhs=zeros[:], start=True, stop=True)
-
-        idle_matmuls(WARM[0], 0)
 
         xv = x.rearrange("b (g u p e) h w -> b g p u (e h w)", g=4, u=2, p=P, e=2)
         wv = [wq.rearrange("(p t) k -> p t k", t=4), wk.rearrange("(p t) k -> p t k", t=4)]
@@ -290,7 +279,6 @@ def tile_guided_cam_module2_pa_kernel(
         for m in range(2):
             transposes(m, 0)
             transposes(m, 1)
-            idle_matmuls(WARM[m + 1], m + 1)
         for i in range(8):
             w_out(i, 0, "s")
             w_out(i, 1, "s")
@@ -324,7 +312,6 @@ def tile_guided_cam_module2_pa_kernel(
                 transposes(i + 2, 1)
                 if i == 0:
                     bn_transposes()
-                    idle_matmuls(WARM[3], 3)
         for m in range(KB, 4):
             passes(1, m)
         for m in range(4):

@@ -18,12 +18,10 @@ AX = mybir.AxisListType
 P = 128
 EPS = 1e-5
 NPOS = 576
-LAST_POOL = (16, 24)
 PIN = True
 CS = (192, 96)
 KB = 3
 EXITS = {4: 2, 5: 1, 6: 1}
-POOLS = {5: 1, 6: 1}
 
 
 def tile_guided_cam_module2_pa_kernel(
@@ -56,8 +54,8 @@ def tile_guided_cam_module2_pa_kernel(
             xt = keep.tile([P, 2, 2 * NPOS], BF16, name="xraw%d" % i)
             nc.sync.dma_start(out=xt[:], in_=xv[i // 4, i % 4])
             xraw.append(xt)
-            if i in (0, 2):
-                for v in range(2 * i, 2 * i + 4):
+            if i in (0, 1):
+                for v in range(4 * i, 4 * i + 4):
                     nc.sync.dma_start(out=bnrows[v : v + 1, :], in_=bnvecs[v].rearrange("(o c) -> o c", o=1))
 
         ident = keep.tile([P, P], F32, name="ident")
@@ -88,24 +86,30 @@ def tile_guided_cam_module2_pa_kernel(
                 nc.tensor.transpose(bank[:, j, :], words[:, j, :], ident[:])
             bnbank[0] = bank
 
-        def bn_first():
-            pairs = bnbank[0][:].rearrange("p j r -> p (j r)").bitcast(BF16)
-            pairs = pairs.rearrange("p (j r e) -> p r j e", j=2, e=2)
-            nc.vector.tensor_copy(out=bnp[:].rearrange("p r (j e) -> p r j e", j=2), in_=pairs[:, 0:8, :, :])
-            nc.vector.tensor_scalar_add(out=sd[:], in0=bnflat[:, 0:8], scalar1=EPS)
+        def bn_first(step):
+            if step == 0:
+                pairs = bnbank[0][:].rearrange("p j r -> p (j r)").bitcast(BF16)
+                pairs = pairs.rearrange("p (j r e) -> p r j e", j=2, e=2)
+                nc.vector.tensor_copy(out=bnp[:].rearrange("p r (j e) -> p r j e", j=2), in_=pairs[:, 0:8, :, :])
+            else:
+                nc.vector.tensor_scalar_add(out=sd[:], in0=bnflat[:, 0:8], scalar1=EPS)
 
         def bn_sqrt():
             nc.scalar.sqrt(sd[:], sd[:])
 
-        def bn_last():
-            nc.vector.reciprocal(out=rstd[:], in_=sd[:])
-            nc.vector.scalar_tensor_tensor(
-                out=a16[:], in0=bnflat[:, 8:16], scalar=1.0 / 16.0, in1=rstd[:], op0=ALU.mult, op1=ALU.mult
-            )
-            nc.vector.tensor_mul(out=ma[:], in0=bnflat[:, 16:24], in1=a16[:])
-            nc.vector.scalar_tensor_tensor(
-                out=c16[:], in0=bnflat[:, 24:32], scalar=1.0 / 16.0, in1=ma[:], op0=ALU.mult, op1=ALU.subtract
-            )
+        def bn_last(step):
+            if step == 0:
+                nc.vector.reciprocal(out=rstd[:], in_=sd[:])
+            elif step == 1:
+                nc.vector.scalar_tensor_tensor(
+                    out=a16[:], in0=bnflat[:, 8:16], scalar=1.0 / 16.0, in1=rstd[:], op0=ALU.mult, op1=ALU.mult
+                )
+            elif step == 2:
+                nc.vector.tensor_mul(out=ma[:], in0=bnflat[:, 16:24], in1=a16[:])
+            else:
+                nc.vector.scalar_tensor_tensor(
+                    out=c16[:], in0=bnflat[:, 24:32], scalar=1.0 / 16.0, in1=ma[:], op0=ALU.mult, op1=ALU.subtract
+                )
 
         tps = {}
         wgs = {}
@@ -267,14 +271,17 @@ def tile_guided_cam_module2_pa_kernel(
             count["out"] = min(count["out"] + n, len(closing))
 
         def pool_next(n):
-            for c, m in closing[count["pooled"] : min(count["pooled"] + n, count["out"])]:
+            for c, m in closing[count["pooled"] : count["pooled"] + n]:
                 pool(c, m)
-                count["pooled"] = count["pooled"] + 1
-                for br in range(2):
-                    if count["pooled"] == LAST_POOL[br]:
-                        for step in ("6", "3r", "3s", "2r", "2s", "1r", "1s"):
-                            fin(step, 4 * br, 4)
-                        store(br)
+            count["pooled"] = count["pooled"] + n
+
+        def fin_vector(m0, n, steps):
+            for step in steps:
+                fin(step, m0, n)
+
+        def fin_scalar(m0, n):
+            for step in ("6", "2s", "3s", "1s"):
+                fin(step, m0, n)
 
         for m in range(2):
             transposes(m, 0)
@@ -283,16 +290,24 @@ def tile_guided_cam_module2_pa_kernel(
             w_out(i, 0, "s")
             w_out(i, 1, "s")
             x_regroup(i, "s")
+            if i == 2:
+                bn_first(0)
+            if i == 3:
+                bn_last(0)
             x_regroup(i, "v")
+            if i == 2:
+                bn_first(1)
+            if i == 3:
+                bn_last(1)
             w_quant(i)
             if i == 2:
-                bn_first()
                 bn_sqrt()
+            if i == 3:
+                bn_last(2)
             x_quant(i)
-            if i == 2:
-                bn_last()
+            if i == 3:
+                bn_last(3)
             leave(EXITS.get(i, 0))
-            pool_next(POOLS.get(i, 0))
             if i < 4:
                 for g in range(i):
                     mx(0, i, g)
@@ -312,14 +327,25 @@ def tile_guided_cam_module2_pa_kernel(
                 transposes(i + 2, 1)
                 if i == 0:
                     bn_transposes()
-        for m in range(KB, 4):
-            passes(1, m)
-        for m in range(4):
+        for m in range(KB):
             passes(2, m)
-        for m in range(4, 8):
+        for m in range(KB, 8):
             passes(1, m)
-        for m in range(4, 8):
             passes(2, m)
-        for n in range(len(closing)):
+        for done in closing[count["out"] :]:
             leave(1)
-            pool_next(1)
+            pool_next(count["out"] - count["pooled"])
+            if done == (2, 3):
+                fin_vector(0, 4, ("2r", "3r"))
+            if done == (1, 4):
+                fin_vector(0, 4, ("1r",))
+            if done == (2, 6):
+                fin_scalar(0, 4)
+                store(0)
+                fin_vector(4, 3, ("2r", "3r"))
+            if done == (1, 7):
+                fin_vector(4, 3, ("1r",))
+        fin_vector(7, 1, ("2r", "3r", "1r"))
+        fin_scalar(4, 3)
+        fin_scalar(7, 1)
+        store(1)

@@ -54,8 +54,8 @@ def tile_guided_cam_module2_pa_kernel(
             xt = keep.tile([P, 2, 2 * NPOS], BF16, name="xraw%d" % i)
             nc.sync.dma_start(out=xt[:], in_=xv[i // 4, i % 4])
             xraw.append(xt)
-            if i in (0, 1):
-                for v in range(4 * i, 4 * i + 4):
+            if i in (0, 2):
+                for v in range(2 * i, 2 * i + 4):
                     nc.sync.dma_start(out=bnrows[v : v + 1, :], in_=bnvecs[v].rearrange("(o c) -> o c", o=1))
 
         ident = keep.tile([P, P], F32, name="ident")

@@ -21,6 +21,7 @@ NPOS = 576
 PIN = True
 CS = (192, 96)
 KB = 3
+GSET = (4, 5, 6, 7)
 EXITS = {4: 2, 5: 1, 6: 1}
 
 
@@ -65,7 +66,13 @@ def tile_guided_cam_module2_pa_kernel(
         ws = [keep.tile([P, 512], U8, name="ws%d" % m, align_bytes=64) for m in range(8)]
         xc = [keep.tile([P, 1152], U32, name="xc%d" % g, align_bytes=64) for g in range(4)]
         xs = [keep.tile([P, 1152], U8, name="xs%d" % g, align_bytes=64) for g in range(4)]
-        z = [keep.tile([P, 2, NPOS], F32, name="z%d" % m) for m in range(8)]
+        zall = keep.tile([P, 8, 2, NPOS], F32, name="zall")
+        z = [zall[:, m, :, :] for m in range(8)]
+        ng = len(GSET)
+        t1 = keep.tile([P, ng, 5, 48], F32, name="t1")
+        t2 = keep.tile([P, ng * 5, 24], F32, name="t2")
+        t3 = keep.tile([P, ng * 30, 2], F32, name="t3")
+        t4 = keep.tile([P, ng, 30], F32, name="t4")
         l6 = keep.tile([P, 8, 2, 36], F32, name="l6")
         res = [keep.tile([P, 2, 4, 50], F32, name="res%d" % br) for br in range(2)]
         a16 = keep.tile([P, 8], F32, name="a16")
@@ -193,7 +200,26 @@ def tile_guided_cam_module2_pa_kernel(
                 out=dst, in_=src, func=ACT.Relu, bias=c16[:, m : m + 1], scale=a16[:, m : m + 1]
             )
 
+        def gpool():
+            g0 = GSET[0]
+            halves = zall[:, g0 : g0 + ng, 0, 0:480].rearrange("p m (hb h r) -> p m hb h r", hb=5, h=2)
+            nc.gpsimd.tensor_tensor(out=t1[:], in0=halves[:, :, :, 0, :], in1=halves[:, :, :, 1, :], op=ALU.add)
+            v1 = t1[:].rearrange("p m hb (h r) -> p (m hb) h r", h=2)
+            nc.gpsimd.tensor_tensor(out=t2[:], in0=v1[:, :, 0, :], in1=v1[:, :, 1, :], op=ALU.add)
+            v2 = t2[:].rearrange("p a (wb h r) -> p (a wb) h r", h=2, r=2)
+            nc.gpsimd.tensor_tensor(out=t3[:], in0=v2[:, :, 0, :], in1=v2[:, :, 1, :], op=ALU.add)
+            v3 = t3[:].rearrange("p (m f) r -> p m f r", m=ng)
+            nc.gpsimd.tensor_tensor(out=t4[:], in0=v3[:, :, :, 0], in1=v3[:, :, :, 1], op=ALU.add)
+
+        def gpool_back():
+            g0 = GSET[0]
+            nc.scalar.copy(out=l6[:, g0 : g0 + ng, 0, 0:30], in_=t4[:])
+
         def pool(c, m):
+            if c == 0 and m in GSET:
+                if m == GSET[-1]:
+                    gpool()
+                return
             if c < 2:
                 src = z[m][:, c, 0:480].rearrange("p (hb hi wb wi) -> p hb wb hi wi", hb=5, hi=4, wb=6, wi=4)
                 dst = l6[:, m, c, 0:30].rearrange("p (hb wb) -> p hb wb", wb=6)
@@ -339,6 +365,8 @@ def tile_guided_cam_module2_pa_kernel(
                 fin_vector(0, 4, ("2r", "3r"))
             if done == (1, 4):
                 fin_vector(0, 4, ("1r",))
+            if done == (2, 5):
+                gpool_back()
             if done == (2, 6):
                 fin_scalar(0, 4)
                 store(0)

@@ -21,6 +21,7 @@ NPOS = 576
 PIN = True
 CS = (192, 96)
 KB = 3
+NL = 2
 GSET = (4, 5, 6, 7)
 EXITS = {4: 2, 5: 1, 6: 1}
 
@@ -343,7 +344,7 @@ def tile_guided_cam_module2_pa_kernel(
                     closing.extend([(0, m) for m in range(4)])
             else:
                 passes(0, i)
-                for g in ((), (0,), (1, 2), (3,))[i - 4]:
+                for g in ((0,), (1,), (2,), (3,))[i - 4]:
                     for m in range(KB):
                         mx(1, m, g)
                 if i == 7:
@@ -355,8 +356,12 @@ def tile_guided_cam_module2_pa_kernel(
                     bn_transposes()
         for m in range(KB):
             passes(2, m)
-        for m in range(KB, 8):
+        for m in range(KB, 8 - NL):
             passes(1, m)
+            passes(2, m)
+        for m in range(8 - NL, 8):
+            passes(1, m)
+        for m in range(8 - NL, 8):
             passes(2, m)
         for done in closing[count["out"] :]:
             leave(1)
@@ -365,15 +370,15 @@ def tile_guided_cam_module2_pa_kernel(
                 fin_vector(0, 4, ("2r", "3r"))
             if done == (1, 4):
                 fin_vector(0, 4, ("1r",))
-            if done == (2, 5):
+            if done == (2, 7 - NL):
                 gpool_back()
-            if done == (2, 6):
                 fin_scalar(0, 4)
                 store(0)
-                fin_vector(4, 3, ("2r", "3r"))
+                fin_vector(4, 4 - NL, ("2r", "3r"))
+            if done == (1, 8 - NL):
+                fin_vector(4, 4 - NL, ("1r",))
             if done == (1, 7):
-                fin_vector(4, 3, ("1r",))
-        fin_vector(7, 1, ("2r", "3r", "1r"))
-        fin_scalar(4, 3)
-        fin_scalar(7, 1)
+                fin_scalar(4, 4 - NL)
+        fin_vector(8 - NL, NL, ("2r", "3r", "1r"))
+        fin_scalar(8 - NL, NL)
         store(1)

@@ -354,15 +354,21 @@ def tile_guided_cam_module2_pa_kernel(
                 transposes(i + 2, 1)
                 if i == 0:
                     bn_transposes()
-        for m in range(KB):
-            passes(2, m)
+        for g in range(4):
+            for m in range(KB):
+                mx(2, m, g)
+        closing.extend([(2, m) for m in range(KB)])
         for m in range(KB, 8 - NL):
-            passes(1, m)
-            passes(2, m)
+            for g in range(4):
+                mx(1, m, g)
+                mx(2, m, g)
+            closing.extend([(1, m), (2, m)])
         for m in range(8 - NL, 8):
             passes(1, m)
-        for m in range(8 - NL, 8):
-            passes(2, m)
+        for g in range(4):
+            for m in range(8 - NL, 8):
+                mx(2, m, g)
+        closing.extend([(2, m) for m in range(8 - NL, 8)])
         for done in closing[count["out"] :]:
             leave(1)
             pool_next(count["out"] - count["pooled"])

from contextlib import ExitStack

import concourse.mybir as mybir
from concourse.masks import make_identity

FLOPS = 2 * 2 * 2 * 512 * 2048 * 576

FP8X4 = mybir.dt.float8_e4m3fn_x4
BF16 = mybir.dt.bfloat16
F32 = mybir.dt.float32
U32 = mybir.dt.uint32
U8 = mybir.dt.uint8
I32 = mybir.dt.int32
ALU = mybir.AluOpType
ACT = mybir.ActivationFunctionType
AX = mybir.AxisListType

P = 128
EPS = 1e-5
NPOS = 576
PIN = True
CS = (192, 96)
KB = 3
NL = 2
GSET = (4, 5, 6, 7)
EXITS = {4: 2, 5: 1, 6: 1}


def tile_guided_cam_module2_pa_kernel(
    tc, x, wq, q_scale, q_bias, q_mean, q_var, wk, k_scale, k_bias, k_mean, k_var, out_0, out_1
):
    nc = tc.nc
    with ExitStack() as ctx:
        keep = ctx.enter_context(tc.tile_pool(name="keep", bufs=1))
        wgrp_pool = ctx.enter_context(tc.tile_pool(name="wgrp", bufs=3))
        xgrp_pool = ctx.enter_context(tc.tile_pool(name="xgrp", bufs=3))
        psum = ctx.enter_context(tc.psum_pool(name="psum", bufs=8))
        if PIN:
            ctx.enter_context(tc.manual_schedule())

        warm = keep.tile([P, 2], F32, name="warm")
        nc.vector.memset(warm[:, 0:1], 1.0)
        nc.scalar.sqrt(warm[:, 1:2], warm[:, 0:1])

        xv = x.rearrange("b (g u p e) h w -> b g p u (e h w)", g=4, u=2, p=P, e=2)
        wv = [wq.rearrange("(p t) k -> p t k", t=4), wk.rearrange("(p t) k -> p t k", t=4)]
        wraw = []
        xraw = []
        bnrows = keep.tile([P, 512], BF16, name="bnrows")
        nc.vector.memset(bnrows[:].bitcast(I32), 0)
        bnvecs = (q_var, k_var, q_scale, k_scale, q_mean, k_mean, q_bias, k_bias)
        for i in range(8):
            wt = keep.tile([P, 2048], BF16, name="wraw%d" % i)
            nc.sync.dma_start(out=wt[:], in_=wv[i // 4][:, i % 4, :])
            wraw.append(wt)
            xt = keep.tile([P, 2, 2 * NPOS], BF16, name="xraw%d" % i)
            nc.sync.dma_start(out=xt[:], in_=xv[i // 4, i % 4])
            xraw.append(xt)
            if i in (0, 2):
                for v in range(2 * i, 2 * i + 4):
                    nc.sync.dma_start(out=bnrows[v : v + 1, :], in_=bnvecs[v].rearrange("(o c) -> o c", o=1))

        ident = keep.tile([P, P], F32, name="ident")
        make_identity(nc, ident[:])

        wc = [keep.tile([P, 512], U32, name="wc%d" % m, align_bytes=64) for m in range(8)]
        ws = [keep.tile([P, 512], U8, name="ws%d" % m, align_bytes=64) for m in range(8)]
        xc = [keep.tile([P, 1152], U32, name="xc%d" % g, align_bytes=64) for g in range(4)]
        xs = [keep.tile([P, 1152], U8, name="xs%d" % g, align_bytes=64) for g in range(4)]
        zall = keep.tile([P, 8, 2, NPOS], F32, name="zall")
        z = [zall[:, m, :, :] for m in range(8)]
        ng = len(GSET)
        t1 = keep.tile([P, ng, 5, 48], F32, name="t1")
        t2 = keep.tile([P, ng * 5, 24], F32, name="t2")
        t3 = keep.tile([P, ng * 30, 2], F32, name="t3")
        t4 = keep.tile([P, ng, 30], F32, name="t4")
        l6 = keep.tile([P, 8, 2, 36], F32, name="l6")
        res = [keep.tile([P, 2, 4, 50], F32, name="res%d" % br) for br in range(2)]
        a16 = keep.tile([P, 8], F32, name="a16")
        c16 = keep.tile([P, 8], F32, name="c16")

        sd = keep.tile([P, 8], F32, name="sd")
        rstd = keep.tile([P, 8], F32, name="rstd")
        ma = keep.tile([P, 8], F32, name="ma")

        bnp = keep.tile([P, 8, 4], F32, name="bnp")
        bnflat = bnp[:].rearrange("p r t -> p (r t)")
        bnbank = {}

        def bn_transposes():
            bank = psum.tile([P, 2, P], F32, name="bnbank", tag="bank")
            words = bnrows[:].bitcast(F32).rearrange("p (c j) -> p j c", j=2)
            for j in range(2):
                nc.tensor.transpose(bank[:, j, :], words[:, j, :], ident[:])
            bnbank[0] = bank

        def bn_first(step):
            if step == 0:
                pairs = bnbank[0][:].rearrange("p j r -> p (j r)").bitcast(BF16)
                pairs = pairs.rearrange("p (j r e) -> p r j e", j=2, e=2)
                nc.vector.tensor_copy(out=bnp[:].rearrange("p r (j e) -> p r j e", j=2), in_=pairs[:, 0:8, :, :])
            else:
                nc.vector.tensor_scalar_add(out=sd[:], in0=bnflat[:, 0:8], scalar1=EPS)

        def bn_sqrt():
            nc.scalar.sqrt(sd[:], sd[:])

        def bn_last(step):
            if step == 0:
                nc.vector.reciprocal(out=rstd[:], in_=sd[:])
            elif step == 1:
                nc.vector.scalar_tensor_tensor(
                    out=a16[:], in0=bnflat[:, 8:16], scalar=1.0 / 16.0, in1=rstd[:], op0=ALU.mult, op1=ALU.mult
                )
            elif step == 2:
                nc.vector.tensor_mul(out=ma[:], in0=bnflat[:, 16:24], in1=a16[:])
            else:
                nc.vector.scalar_tensor_tensor(
                    out=c16[:], in0=bnflat[:, 24:32], scalar=1.0 / 16.0, in1=ma[:], op0=ALU.mult, op1=ALU.subtract
                )

        tps = {}
        wgs = {}
        xgs = {}
        ys = {}

        def transposes(m, h):
            w32 = wraw[m][:].bitcast(F32)
            tp = psum.tile([P, 4, P], F32, name="tp%d_%d" % (m, h), tag="bank")
            for j in range(4):
                blk = 4 * h + j
                nc.tensor.transpose(tp[:, j, :], w32[:, P * blk : P * (blk + 1)], ident[:])
            tps[(m, h)] = tp

        def w_out(m, h, engine):
            if m not in wgs:
                wgs[m] = wgrp_pool.tile([P, 2048], BF16, name="wg%d" % m, tag="wg", align_bytes=64)
            wg32 = wgs[m][:].bitcast(F32).rearrange("p (g c u) -> p g c u", g=4, c=P, u=2)
            src = tps[(m, h)][:].rearrange("p (g u) c -> p g c u", u=2)
            dst = wg32[:, 2 * h : 2 * h + 2, :, :]
            if engine == "v":
                nc.vector.tensor_copy(out=dst, in_=src)
            else:
                nc.scalar.copy(out=dst, in_=src)

        def w_quant(m):
            nc.vector.quantize_mx(out=wc[m][:].bitcast(FP8X4), scales=ws[m][:], in_=wgs[m][:])

        def x_regroup(i, engine):
            b = i // 4
            if i not in xgs:
                xgs[i] = xgrp_pool.tile([P, NPOS, 4], BF16, name="xg%d" % i, tag="xg", align_bytes=64)
            cv = NPOS - CS[b]
            lo, hi = (0, cv) if engine == "v" else (cv, NPOS)
            if lo == hi:
                return
            src = xraw[i][:].rearrange("p u (e n) -> p (u e) n", e=2)[:, :, lo:hi]
            src = src.rearrange("p t (c i) -> p c t i", i=4)
            dst = xgs[i][:, lo:hi, :].rearrange("p (c i) t -> p c t i", i=4)
            if engine == "v":
                nc.vector.tensor_copy(out=dst, in_=src)
            else:
                nc.scalar.copy(out=dst, in_=src)

        def x_quant(i):
            b, g = i // 4, i % 4
            flat = xgs[i][:].rearrange("p c t -> p (c t)")
            nc.vector.quantize_mx(
                out=xc[g][:, 512 * b : 512 * b + 512].bitcast(FP8X4),
                scales=xs[g][:, 512 * b : 512 * b + 512],
                in_=flat[:, 0:2048],
            )
            nc.vector.quantize_mx(
                out=xc[g][:, 1024 + 64 * b : 1088 + 64 * b].bitcast(FP8X4),
                scales=xs[g][:, 1024 + 64 * b : 1088 + 64 * b],
                in_=flat[:, 2048:2304],
            )

        def mx(c, m, g):
            lo, n = ((0, 512), (512, 512), (1024, 128))[c]
            if g == 0:
                ys[(c, m)] = psum.tile([P, n], F32, name="y%d_%d" % (c, m), tag="bank")
            nc.tensor.matmul_mx(
                out=ys[(c, m)][:],
                lhsT=wc[m][:, P * g : P * (g + 1)].bitcast(FP8X4),
                lhsT_scale=ws[m][:, P * g : P * (g + 1)],
                rhs=xc[g][:, lo : lo + n].bitcast(FP8X4),
                rhs_scale=xs[g][:, lo : lo + n],
                start=(g == 0),
                stop=(g == 3),
            )

        def y_out(c, m):
            if c < 2:
                dst = z[m][:, c, 0:512]
                src = ys[(c, m)][:]
            else:
                dst = z[m][:, :, 512:NPOS]
                src = ys[(c, m)][:].rearrange("p (b n) -> p b n", b=2)
            nc.scalar.activation(
                out=dst, in_=src, func=ACT.Relu, bias=c16[:, m : m + 1], scale=a16[:, m : m + 1]
            )

        def gpool():
            g0 = GSET[0]
            halves = zall[:, g0 : g0 + ng, 0, 0:480].rearrange("p m (hb h r) -> p m hb h r", hb=5, h=2)
            nc.gpsimd.tensor_tensor(out=t1[:], in0=halves[:, :, :, 0, :], in1=halves[:, :, :, 1, :], op=ALU.add)
            v1 = t1[:].rearrange("p m hb (h r) -> p (m hb) h r", h=2)
            nc.gpsimd.tensor_tensor(out=t2[:], in0=v1[:, :, 0, :], in1=v1[:, :, 1, :], op=ALU.add)
            v2 = t2[:].rearrange("p a (wb h r) -> p (a wb) h r", h=2, r=2)
            nc.gpsimd.tensor_tensor(out=t3[:], in0=v2[:, :, 0, :], in1=v2[:, :, 1, :], op=ALU.add)
            v3 = t3[:].rearrange("p (m f) r -> p m f r", m=ng)
            nc.gpsimd.tensor_tensor(out=t4[:], in0=v3[:, :, :, 0], in1=v3[:, :, :, 1], op=ALU.add)

        def gpool_back():
            g0 = GSET[0]
            nc.scalar.copy(out=l6[:, g0 : g0 + ng, 0, 0:30], in_=t4[:])

        def pool(c, m):
            if c == 0 and m in GSET:
                if m == GSET[-1]:
                    gpool()
                return
            if c < 2:
                src = z[m][:, c, 0:480].rearrange("p (hb hi wb wi) -> p hb wb hi wi", hb=5, hi=4, wb=6, wi=4)
                dst = l6[:, m, c, 0:30].rearrange("p (hb wb) -> p hb wb", wb=6)
            else:
                src = z[m][:, :, 480:NPOS].rearrange("p b (hi wb wi) -> p b wb hi wi", hi=4, wb=6, wi=4)
                dst = l6[:, m, :, 30:36]
            nc.vector.tensor_reduce(out=dst, in_=src, axis=AX.XY, op=ALU.add)

        sums = {}

        def fin(step, m0, n):
            br, t0 = m0 // 4, m0 % 4
            part = l6[:, m0 : m0 + n, :, :]
            out_view = res[br][:].rearrange("p b t f -> p t b f")[:, t0 : t0 + n, :, :]
            if step == "6":
                nc.scalar.copy(out=out_view[:, :, :, 14:50], in_=part)
            elif step == "3r":
                sums[(3, m0)] = keep.tile([P, 6 * n, 3], F32, name="s3_%d" % m0)
                nc.vector.tensor_reduce(
                    out=sums[(3, m0)][:],
                    in_=part.rearrange("p m b (i di j dj) -> p (m b i) j di dj", i=3, di=2, j=3, dj=2),
                    axis=AX.XY,
                    op=ALU.add,
                )
            elif step == "3s":
                nc.scalar.mul(
                    out_view[:, :, :, 5:14],
                    sums[(3, m0)][:].rearrange("p (m b i) j -> p m b (i j)", m=n, b=2),
                    0.25,
                )
            elif step == "2r":
                sums[(2, m0)] = keep.tile([P, 4 * n, 2], F32, name="s2_%d" % m0)
                nc.vector.tensor_reduce(
                    out=sums[(2, m0)][:],
                    in_=part.rearrange("p m b (i di j dj) -> p (m b i) j di dj", i=2, di=3, j=2, dj=3),
                    axis=AX.XY,
                    op=ALU.add,
                )
            elif step == "2s":
                nc.scalar.mul(
                    out_view[:, :, :, 1:5],
                    sums[(2, m0)][:].rearrange("p (m b i) j -> p m b (i j)", m=n, b=2),
                    1.0 / 9.0,
                )
            elif step == "1r":
                sums[(1, m0)] = keep.tile([P, 2 * n], F32, name="s1_%d" % m0)
                nc.vector.tensor_reduce(
                    out=sums[(1, m0)][:],
                    in_=sums[(2, m0)][:].rearrange("p (mb i) j -> p mb (i j)", i=2),
                    axis=AX.X,
                    op=ALU.add,
                )
            else:
                nc.scalar.mul(
                    out_view[:, :, :, 0:1],
                    sums[(1, m0)][:].rearrange("p (m b o) -> p m b o", m=n, o=1),
                    1.0 / 36.0,
                )

        def store(br):
            dram = (out_0, out_1)[br].rearrange("b (p t) f -> p b (t f)", t=4)
            nc.sync.dma_start(out=dram, in_=res[br][:].rearrange("p b t f -> p b (t f)"))

        closing = []
        count = {"out": 0, "pooled": 0}

        def passes(c, m):
            for g in range(4):
                mx(c, m, g)
            closing.append((c, m))

        def leave(n):
            for c, m in closing[count["out"] : count["out"] + n]:
                y_out(c, m)
            count["out"] = min(count["out"] + n, len(closing))

        def pool_next(n):
            for c, m in closing[count["pooled"] : count["pooled"] + n]:
                pool(c, m)
            count["pooled"] = count["pooled"] + n

        def fin_vector(m0, n, steps):
            for step in steps:
                fin(step, m0, n)

        def fin_scalar(m0, n):
            for step in ("6", "2s", "3s", "1s"):
                fin(step, m0, n)

        for m in range(2):
            transposes(m, 0)
            transposes(m, 1)
        for i in range(8):
            w_out(i, 0, "s")
            w_out(i, 1, "s")
            x_regroup(i, "s")
            if i == 2:
                bn_first(0)
            if i == 3:
                bn_last(0)
            x_regroup(i, "v")
            if i == 2:
                bn_first(1)
            if i == 3:
                bn_last(1)
            w_quant(i)
            if i == 2:
                bn_sqrt()
            if i == 3:
                bn_last(2)
            x_quant(i)
            if i == 3:
                bn_last(3)
            leave(EXITS.get(i, 0))
            if i < 4:
                for g in range(i):
                    mx(0, i, g)
                for m in range(i + 1):
                    mx(0, m, i)
                if i == 3:
                    closing.extend([(0, m) for m in range(4)])
            else:
                passes(0, i)
                for g in ((0,), (1,), (2,), (3,))[i - 4]:
                    for m in range(KB):
                        mx(1, m, g)
                if i == 7:
                    closing.extend([(1, m) for m in range(KB)])
            if i < 6:
                transposes(i + 2, 0)
                transposes(i + 2, 1)
                if i == 0:
                    bn_transposes()
        for g in range(4):
            for m in range(KB):
                mx(2, m, g)
        closing.extend([(2, m) for m in range(KB)])
        for m in range(KB, 8 - NL):
            for g in range(4):
                mx(1, m, g)
                mx(2, m, g)
            closing.extend([(1, m), (2, m)])
        for m in range(8 - NL, 8):
            passes(1, m)
        for g in range(4):
            for m in range(8 - NL, 8):
                mx(2, m, g)
        closing.extend([(2, m) for m in range(8 - NL, 8)])
        for done in closing[count["out"] :]:
            leave(1)
            pool_next(count["out"] - count["pooled"])
            if done == (2, 3):
                fin_vector(0, 4, ("2r", "3r"))
            if done == (1, 4):
                fin_vector(0, 4, ("1r",))
            if done == (2, 7 - NL):
                gpool_back()
                fin_scalar(0, 4)
                store(0)
                fin_vector(4, 4 - NL, ("2r", "3r"))
            if done == (1, 8 - NL):
                fin_vector(4, 4 - NL, ("1r",))
            if done == (1, 7):
                fin_scalar(4, 4 - NL)
        fin_vector(8 - NL, NL, ("2r", "3r", "1r"))
        fin_scalar(8 - NL, NL)
        store(1)
